import numpy as np
import ml_dtypes


def mxq(x, axis, fmt="e4m3"):
    dtype, down = {"e4m3": (ml_dtypes.float8_e4m3fn, 7), "e5m2": (ml_dtypes.float8_e5m2, 14)}[fmt]
    v = np.moveaxis(np.asarray(x, np.float32).astype(ml_dtypes.bfloat16).astype(np.float64), axis, -1)
    blocks = v.reshape(v.shape[:-1] + (-1, 32))
    amax = np.abs(blocks).max(-1, keepdims=True)
    byte = np.maximum(np.where(amax > 0, np.frexp(amax)[1] - 1 + 127, 0) - down, 1)
    scale = np.exp2(byte - 127.0)
    codes = (blocks / scale).astype(np.float32).astype(dtype).astype(np.float64)
    return np.moveaxis((codes * scale).reshape(v.shape), -1, axis)


WIDE = False


def mx_kscale(k):
    if not WIDE:
        return np.ones(k)
    levels = np.array([10, -10, 5, -5, 0])
    if k % 512:
        return np.exp2(np.random.permutation(np.resize(levels, k // 32))).repeat(32)
    a = np.empty((k // 512, 16))
    for p in range(k // 512):
        a[p, :8] = np.random.permutation(np.resize(levels, 8))
        for g in range(8):
            far = levels[np.abs(levels - a[p, g]) >= 10]
            a[p, g + 8] = far[np.random.randint(len(far))]
    return np.exp2(a.ravel()).repeat(32)


BF16 = ml_dtypes.bfloat16


def bf(x):
    return np.asarray(x, np.float32).astype(BF16)


def f64(x):
    return np.asarray(x).astype(np.float64)


B, L, F, D, N = 16, 1024, 512, 512, 8192
TOP = 0.8 * np.sqrt(2.0 * np.log(L))


def elu(v):
    return np.where(v > 0.0, v, np.exp(np.minimum(v, 0.0)) - 1.0)


def setup_inputs():
    s = mx_kscale(F)
    return {"x": bf(np.random.standard_normal((B, L, F)) * s),
            "conv_w": bf(np.random.standard_normal((D, F)) / np.sqrt(F) / s),
            "conv_b": bf(np.random.standard_normal(D) * 2.0 - TOP)}


def reference(x, conv_w, conv_b):
    z = (mxq(f64(x), 2, "e4m3") @ mxq(f64(conv_w), 1, "e4m3").T) + f64(conv_b)
    return elu(z).max(axis=1)

@@ -1,0 +1,241 @@
+from contextlib import ExitStack
+
+import concourse.mybir as mybir
+from concourse.masks import make_identity
+
+F32 = mybir.dt.float32
+BF16 = mybir.dt.bfloat16
+U32 = mybir.dt.uint32
+U8 = mybir.dt.uint8
+FP8X4 = mybir.dt.float8_e4m3fn_x4
+ALU = mybir.AluOpType
+FUNC = mybir.ActivationFunctionType
+
+P = 128
+PACK = 4
+FEATURES = P * PACK
+BATCH = 16
+POSITIONS = 1024
+CHANNELS = 512
+CHANNEL_TILES = CHANNELS // P
+CHUNK = 512
+CHUNK_ROW_TILES = CHUNK // P
+N_CHUNKS = BATCH * POSITIONS // CHUNK
+PAIR = 2 * P
+PSUM_BANKS = 8
+N_PAIRED = 2
+N_PLAIN = CHANNEL_TILES - N_PAIRED
+
+FLOPS = 2 * BATCH * POSITIONS * FEATURES * CHANNELS
+
+
+def flip_rows(nc, psum, ident, rows, grouped, n_row_tiles):
+    row_words = rows.bitcast(F32)
+    grouped_words = grouped.bitcast(F32)
+    for pair in range(n_row_tiles // 2):
+        flipped = psum.tile([P, 2, PAIR], F32, name="bank")
+        for s in range(2):
+            for u in range(2):
+                nc.tensor.transpose(
+                    flipped[:, u, s * P : (s + 1) * P],
+                    row_words[:, 2 * pair + s, u : 2 * P : 2],
+                    ident,
+                )
+        nc.scalar.copy(
+            out=grouped_words[:, pair * PAIR : (pair + 1) * PAIR, :],
+            in_=flipped[:].rearrange("p u r -> p r u"),
+        )
+
+
+def quantise(nc, grouped, codes, scales):
+    nc.vector.quantize_mx(
+        out=codes.bitcast(FP8X4),
+        scales=scales,
+        in_=grouped.rearrange("p r j -> p (r j)"),
+    )
+
+
+def tile_conceptembedmodel_pa_t_kernel(tc, x, conv_w, conv_b, out):
+    nc = tc.nc
+    x_rows = x.flatten_outer_dims()
+
+    with ExitStack() as ctx:
+        consts = ctx.enter_context(tc.tile_pool(name="consts", bufs=1))
+        x_pool = ctx.enter_context(tc.tile_pool(name="x_pool", bufs=N_CHUNKS))
+        stage = ctx.enter_context(tc.tile_pool(name="stage", bufs=4))
+        pair_in = ctx.enter_context(tc.tile_pool(name="pair_in", bufs=4))
+        pair_out = ctx.enter_context(tc.tile_pool(name="pair_out", bufs=2))
+        psum = ctx.enter_context(tc.psum_pool(name="psum", bufs=PSUM_BANKS))
+        ctx.enter_context(tc.manual_schedule())
+
+        w_rows = consts.tile([P, CHANNEL_TILES, FEATURES], BF16)
+        nc.sync.dma_start(out=w_rows[:], in_=conv_w.rearrange("(t p) f -> p t f", p=P))
+        x_chunks = []
+        for c in range(N_CHUNKS):
+            x_chunk = x_pool.tile([P, CHUNK_ROW_TILES, FEATURES], BF16, name="x_chunk")
+            nc.sync.dma_start(
+                out=x_chunk[:],
+                in_=x_rows[c * CHUNK : (c + 1) * CHUNK, :].rearrange(
+                    "(p j) f -> p j f", j=CHUNK_ROW_TILES
+                ),
+            )
+            x_chunks.append(x_chunk)
+        bias_rows = consts.tile([P, P], BF16)
+        nc.vector.memset(bias_rows[:], 0.0)
+        nc.scalar.dma_start(
+            out=bias_rows[0:CHANNEL_TILES, :], in_=conv_b.rearrange("(t j) -> t j", j=P)
+        )
+
+        ident = consts.tile([P, P], F32)
+        make_identity(nc, ident[:])
+        warm = consts.tile([P, 1], F32)
+        nc.vector.memset(warm[:], 0.0)
+        nc.scalar.activation(out=warm[:], in_=warm[:], func=FUNC.Exp)
+        result = consts.tile([P, P], F32)
+        nc.vector.memset(result[:], 0.0)
+        bias_rows_f32 = consts.tile([P, P], F32)
+        nc.vector.tensor_copy(out=bias_rows_f32[:], in_=bias_rows[:])
+
+        w_grouped = consts.tile([P, CHANNELS, PACK], BF16, align_bytes=64)
+        w_codes = consts.tile([P, CHANNELS], U32, align_bytes=64)
+        w_scales = consts.tile([P, CHANNELS], U8, align_bytes=64)
+        flip_rows(nc, psum, ident[:], w_rows[:], w_grouped[:], CHANNEL_TILES)
+        quantise(nc, w_grouped[:], w_codes[:], w_scales[:])
+        neg_grouped = consts.tile([P, N_PAIRED * P, PACK], BF16, align_bytes=64)
+        neg_codes = consts.tile([P, N_PAIRED * P], U32, align_bytes=64)
+        neg_scales = consts.tile([P, N_PAIRED * P], U8, align_bytes=64)
+
+        grouped_of = {}
+        codes_of = {}
+        scales_of = {}
+        excess_of = {}
+        second_of = {}
+        larger_of = {}
+        plain_max = consts.tile([P, N_CHUNKS, N_PLAIN], F32)
+        seq_max = consts.tile([P, BATCH, CHANNEL_TILES], F32)
+
+        def flip_chunk(c):
+            grouped_of[c] = stage.tile([P, CHUNK, PACK], BF16, align_bytes=64, name="x_grouped")
+            flip_rows(nc, psum, ident[:], x_chunks[c][:], grouped_of[c][:], CHUNK_ROW_TILES)
+
+        def quantise_chunk(c):
+            codes_of[c] = stage.tile([P, CHUNK], U32, align_bytes=64, name="x_codes")
+            scales_of[c] = stage.tile([P, CHUNK], U8, align_bytes=64, name="x_scales")
+            quantise(nc, grouped_of[c][:], codes_of[c][:], scales_of[c][:])
+
+        def mx_pass(acc, weight_codes, weight_scales, c, start, stop):
+            nc.tensor.matmul_mx(
+                out=acc,
+                lhsT=weight_codes.bitcast(FP8X4),
+                lhsT_scale=weight_scales,
+                rhs=codes_of[c][:].bitcast(FP8X4),
+                rhs_scale=scales_of[c][:],
+                start=start,
+                stop=stop,
+            )
+
+        def multiply_plain(c):
+            for t in range(N_PLAIN):
+                channels = slice(t * P, (t + 1) * P)
+                acc = psum.tile([P, CHUNK], F32, name="bank")
+                mx_pass(acc[:], w_codes[:, channels], w_scales[:, channels], c, True, True)
+                nc.vector.tensor_reduce(
+                    out=plain_max[:, c, t : t + 1],
+                    in_=acc[:],
+                    axis=mybir.AxisListType.X,
+                    op=ALU.max,
+                )
+
+        def multiply_paired(b, i):
+            first, second = 2 * b, 2 * b + 1
+            channels = slice((N_PLAIN + i) * P, (N_PLAIN + i + 1) * P)
+            negated = slice(i * P, (i + 1) * P)
+            difference = psum.tile([P, CHUNK], F32, name="bank")
+            mx_pass(difference[:], w_codes[:, channels], w_scales[:, channels], first, True, False)
+            mx_pass(difference[:], neg_codes[:, negated], neg_scales[:, negated], second, False, True)
+            products = psum.tile([P, CHUNK], F32, name="bank")
+            mx_pass(products[:], w_codes[:, channels], w_scales[:, channels], second, True, True)
+            excess_of[b, i] = pair_in.tile([P, CHUNK], F32, name="excess")
+            second_of[b, i] = pair_in.tile([P, CHUNK], F32, name="second_products")
+            nc.scalar.activation(out=excess_of[b, i][:], in_=difference[:], func=FUNC.Relu)
+            nc.scalar.copy(out=second_of[b, i][:], in_=products[:])
+
+        def add_paired(b, i):
+            larger_of[b, i] = pair_out.tile([P, CHUNK], F32, name="larger_%d" % i)
+            nc.gpsimd.tensor_tensor(
+                out=larger_of[b, i][:], in0=second_of[b, i][:], in1=excess_of[b, i][:], op=ALU.add
+            )
+
+        def reduce_paired(b, i):
+            nc.vector.tensor_reduce(
+                out=seq_max[:, b, N_PLAIN + i : N_PLAIN + i + 1],
+                in_=larger_of[b, i][:],
+                axis=mybir.AxisListType.X,
+                op=ALU.max,
+            )
+
+        flip_chunk(0)
+        flip_chunk(1)
+        quantise_chunk(0)
+        quantise_chunk(1)
+        multiply_plain(0)
+        nc.vector.tensor_scalar_mul(
+            out=neg_grouped[:], in0=w_grouped[:, N_PLAIN * P :, :], scalar1=-1.0
+        )
+        quantise(nc, neg_grouped[:], neg_codes[:], neg_scales[:])
+        flip_chunk(2)
+        flip_chunk(3)
+        bias_flipped = psum.tile([P, 2, PAIR], F32, name="bank")
+        nc.tensor.transpose(bias_flipped[:, 0, 0:P], bias_rows_f32[:], ident[:])
+        bias_col = consts.tile([P, CHANNEL_TILES], F32)
+        nc.scalar.copy(out=bias_col[:], in_=bias_flipped[:, 0, 0:CHANNEL_TILES])
+        for b in range(BATCH):
+            for i in range(N_PAIRED):
+                multiply_paired(b, i)
+            if b + 1 < BATCH:
+                quantise_chunk(2 * b + 2)
+                quantise_chunk(2 * b + 3)
+            for i in range(N_PAIRED):
+                if b >= 1:
+                    reduce_paired(b - 1, i)
+                add_paired(b, i)
+            multiply_plain(2 * b + 1)
+            if b + 1 < BATCH:
+                multiply_plain(2 * b + 2)
+            if b + 2 < BATCH:
+                flip_chunk(2 * b + 4)
+                flip_chunk(2 * b + 5)
+        for i in range(N_PAIRED):
+            reduce_paired(BATCH - 1, i)
+
+        halves = plain_max[:].rearrange("p (b h) t -> p b h t", h=2)
+        nc.vector.tensor_tensor(
+            out=seq_max[:, :, 0:N_PLAIN], in0=halves[:, :, 0, :], in1=halves[:, :, 1, :], op=ALU.max
+        )
+        shape = [P, BATCH, CHANNEL_TILES]
+        v = consts.tile(shape, F32)
+        nc.vector.tensor_tensor(
+            out=v[:], in0=seq_max[:], in1=bias_col[:].unsqueeze(1).to_broadcast(shape), op=ALU.add
+        )
+        negative = consts.tile(shape, F32)
+        nc.vector.tensor_scalar_min(out=negative[:], in0=v[:], scalar1=0.0)
+        nc.scalar.activation(out=negative[:], in_=negative[:], func=FUNC.Exp)
+        positive = consts.tile(shape, F32)
+        nc.vector.tensor_scalar_max(out=positive[:], in0=v[:], scalar1=0.0)
+        nc.vector.scalar_tensor_tensor(
+            out=result[:, 0 : BATCH * CHANNEL_TILES],
+            in0=negative[:].rearrange("p b t -> p (b t)"),
+            scalar=-1.0,
+            in1=positive[:].rearrange("p b t -> p (b t)"),
+            op0=ALU.add,
+            op1=ALU.add,
+        )
+
+        result_flipped = psum.tile([P, 2, PAIR], F32, name="bank")
+        nc.tensor.transpose(result_flipped[:, 0, 0:P], result[:], ident[:])
+        out_rows = consts.tile([P, P], F32)
+        nc.scalar.copy(out=out_rows[:], in_=result_flipped[:, 0, 0:P])
+        nc.sync.dma_start(
+            out=out.rearrange("b (t j) -> (b t) j", j=P),
+            in_=out_rows[0 : BATCH * CHANNEL_TILES, :],
+        )

@@ -25,22 +25,24 @@ PAIR = 2 * P
 PSUM_BANKS = 8
 N_PAIRED = 2
 N_PLAIN = CHANNEL_TILES - N_PAIRED
+N_SORTED = 2
 
 FLOPS = 2 * BATCH * POSITIONS * FEATURES * CHANNELS
 
 
-def flip_rows(nc, psum, ident, rows, grouped, n_row_tiles):
+def flip_rows(nc, psum, ident, rows, grouped, n_row_tiles, sorted_rows):
     row_words = rows.bitcast(F32)
     grouped_words = grouped.bitcast(F32)
     for pair in range(n_row_tiles // 2):
         flipped = psum.tile([P, 2, PAIR], F32, name="bank")
         for s in range(2):
+            t = 2 * pair + s
             for u in range(2):
-                nc.tensor.transpose(
-                    flipped[:, u, s * P : (s + 1) * P],
-                    row_words[:, 2 * pair + s, u : 2 * P : 2],
-                    ident,
-                )
+                if t in sorted_rows:
+                    words = sorted_rows[t][:, u, :]
+                else:
+                    words = row_words[:, t, u : 2 * P : 2]
+                nc.tensor.transpose(flipped[:, u, s * P : (s + 1) * P], words, ident)
         nc.scalar.copy(
             out=grouped_words[:, pair * PAIR : (pair + 1) * PAIR, :],
             in_=flipped[:].rearrange("p u r -> p r u"),
@@ -63,6 +65,7 @@ def tile_conceptembedmodel_pa_t_kernel(tc, x, conv_w, conv_b, out):
         consts = ctx.enter_context(tc.tile_pool(name="consts", bufs=1))
         x_pool = ctx.enter_context(tc.tile_pool(name="x_pool", bufs=N_CHUNKS))
         stage = ctx.enter_context(tc.tile_pool(name="stage", bufs=4))
+        sort_pool = ctx.enter_context(tc.tile_pool(name="sort_pool", bufs=2 * N_SORTED))
         pair_in = ctx.enter_context(tc.tile_pool(name="pair_in", bufs=4))
         pair_out = ctx.enter_context(tc.tile_pool(name="pair_out", bufs=2))
         psum = ctx.enter_context(tc.psum_pool(name="psum", bufs=PSUM_BANKS))
@@ -99,12 +102,13 @@ def tile_conceptembedmodel_pa_t_kernel(tc, x, conv_w, conv_b, out):
         w_grouped = consts.tile([P, CHANNELS, PACK], BF16, align_bytes=64)
         w_codes = consts.tile([P, CHANNELS], U32, align_bytes=64)
         w_scales = consts.tile([P, CHANNELS], U8, align_bytes=64)
-        flip_rows(nc, psum, ident[:], w_rows[:], w_grouped[:], CHANNEL_TILES)
+        flip_rows(nc, psum, ident[:], w_rows[:], w_grouped[:], CHANNEL_TILES, {})
         quantise(nc, w_grouped[:], w_codes[:], w_scales[:])
         neg_grouped = consts.tile([P, N_PAIRED * P, PACK], BF16, align_bytes=64)
         neg_codes = consts.tile([P, N_PAIRED * P], U32, align_bytes=64)
         neg_scales = consts.tile([P, N_PAIRED * P], U8, align_bytes=64)
 
+        sorted_of = {}
         grouped_of = {}
         codes_of = {}
         scales_of = {}
@@ -114,9 +118,26 @@ def tile_conceptembedmodel_pa_t_kernel(tc, x, conv_w, conv_b, out):
         plain_max = consts.tile([P, N_CHUNKS, N_PLAIN], F32)
         seq_max = consts.tile([P, BATCH, CHANNEL_TILES], F32)
 
+        def sort_chunk(c):
+            sorted_of[c] = {}
+            for t in range(N_SORTED):
+                sorted_of[c][t] = sort_pool.tile([P, 2, P], F32, name="sorted_words")
+                nc.gpsimd.tensor_copy(
+                    out=sorted_of[c][t][:],
+                    in_=x_chunks[c][:, t, :].bitcast(F32).rearrange("p (m u) -> p u m", u=2),
+                )
+
         def flip_chunk(c):
             grouped_of[c] = stage.tile([P, CHUNK, PACK], BF16, align_bytes=64, name="x_grouped")
-            flip_rows(nc, psum, ident[:], x_chunks[c][:], grouped_of[c][:], CHUNK_ROW_TILES)
+            flip_rows(
+                nc,
+                psum,
+                ident[:],
+                x_chunks[c][:],
+                grouped_of[c][:],
+                CHUNK_ROW_TILES,
+                sorted_of.get(c, {}),
+            )
 
         def quantise_chunk(c):
             codes_of[c] = stage.tile([P, CHUNK], U32, align_bytes=64, name="x_codes")
@@ -190,6 +211,8 @@ def tile_conceptembedmodel_pa_t_kernel(tc, x, conv_w, conv_b, out):
         bias_col = consts.tile([P, CHANNEL_TILES], F32)
         nc.scalar.copy(out=bias_col[:], in_=bias_flipped[:, 0, 0:CHANNEL_TILES])
         for b in range(BATCH):
+            if b + 2 < BATCH:
+                sort_chunk(2 * b + 5)
             for i in range(N_PAIRED):
                 multiply_paired(b, i)
             if b + 1 < BATCH:

from contextlib import ExitStack

import concourse.mybir as mybir
from concourse.masks import make_identity

F32 = mybir.dt.float32
BF16 = mybir.dt.bfloat16
U32 = mybir.dt.uint32
U8 = mybir.dt.uint8
FP8X4 = mybir.dt.float8_e4m3fn_x4
ALU = mybir.AluOpType
FUNC = mybir.ActivationFunctionType

P = 128
PACK = 4
FEATURES = P * PACK
BATCH = 16
POSITIONS = 1024
CHANNELS = 512
CHANNEL_TILES = CHANNELS // P
CHUNK = 512
CHUNK_ROW_TILES = CHUNK // P
N_CHUNKS = BATCH * POSITIONS // CHUNK
PAIR = 2 * P
PSUM_BANKS = 8
N_PAIRED = 2
N_PLAIN = CHANNEL_TILES - N_PAIRED
N_SORTED = 2

FLOPS = 2 * BATCH * POSITIONS * FEATURES * CHANNELS


def flip_rows(nc, psum, ident, rows, grouped, n_row_tiles, sorted_rows):
    row_words = rows.bitcast(F32)
    grouped_words = grouped.bitcast(F32)
    for pair in range(n_row_tiles // 2):
        flipped = psum.tile([P, 2, PAIR], F32, name="bank")
        for s in range(2):
            t = 2 * pair + s
            for u in range(2):
                if t in sorted_rows:
                    words = sorted_rows[t][:, u, :]
                else:
                    words = row_words[:, t, u : 2 * P : 2]
                nc.tensor.transpose(flipped[:, u, s * P : (s + 1) * P], words, ident)
        nc.scalar.copy(
            out=grouped_words[:, pair * PAIR : (pair + 1) * PAIR, :],
            in_=flipped[:].rearrange("p u r -> p r u"),
        )


def quantise(nc, grouped, codes, scales):
    nc.vector.quantize_mx(
        out=codes.bitcast(FP8X4),
        scales=scales,
        in_=grouped.rearrange("p r j -> p (r j)"),
    )


def tile_conceptembedmodel_pa_t_kernel(tc, x, conv_w, conv_b, out):
    nc = tc.nc
    x_rows = x.flatten_outer_dims()

    with ExitStack() as ctx:
        consts = ctx.enter_context(tc.tile_pool(name="consts", bufs=1))
        x_pool = ctx.enter_context(tc.tile_pool(name="x_pool", bufs=N_CHUNKS))
        stage = ctx.enter_context(tc.tile_pool(name="stage", bufs=4))
        sort_pool = ctx.enter_context(tc.tile_pool(name="sort_pool", bufs=2 * N_SORTED))
        pair_in = ctx.enter_context(tc.tile_pool(name="pair_in", bufs=4))
        pair_out = ctx.enter_context(tc.tile_pool(name="pair_out", bufs=2))
        psum = ctx.enter_context(tc.psum_pool(name="psum", bufs=PSUM_BANKS))
        ctx.enter_context(tc.manual_schedule())

        w_rows = consts.tile([P, CHANNEL_TILES, FEATURES], BF16)
        nc.sync.dma_start(out=w_rows[:], in_=conv_w.rearrange("(t p) f -> p t f", p=P))
        x_chunks = []
        for c in range(N_CHUNKS):
            x_chunk = x_pool.tile([P, CHUNK_ROW_TILES, FEATURES], BF16, name="x_chunk")
            nc.sync.dma_start(
                out=x_chunk[:],
                in_=x_rows[c * CHUNK : (c + 1) * CHUNK, :].rearrange(
                    "(p j) f -> p j f", j=CHUNK_ROW_TILES
                ),
            )
            x_chunks.append(x_chunk)
        bias_rows = consts.tile([P, P], BF16)
        nc.vector.memset(bias_rows[:], 0.0)
        nc.scalar.dma_start(
            out=bias_rows[0:CHANNEL_TILES, :], in_=conv_b.rearrange("(t j) -> t j", j=P)
        )

        ident = consts.tile([P, P], F32)
        make_identity(nc, ident[:])
        warm = consts.tile([P, 1], F32)
        nc.vector.memset(warm[:], 0.0)
        nc.scalar.activation(out=warm[:], in_=warm[:], func=FUNC.Exp)
        result = consts.tile([P, P], F32)
        nc.vector.memset(result[:], 0.0)
        bias_rows_f32 = consts.tile([P, P], F32)
        nc.vector.tensor_copy(out=bias_rows_f32[:], in_=bias_rows[:])

        w_grouped = consts.tile([P, CHANNELS, PACK], BF16, align_bytes=64)
        w_codes = consts.tile([P, CHANNELS], U32, align_bytes=64)
        w_scales = consts.tile([P, CHANNELS], U8, align_bytes=64)
        flip_rows(nc, psum, ident[:], w_rows[:], w_grouped[:], CHANNEL_TILES, {})
        quantise(nc, w_grouped[:], w_codes[:], w_scales[:])
        neg_grouped = consts.tile([P, N_PAIRED * P, PACK], BF16, align_bytes=64)
        neg_codes = consts.tile([P, N_PAIRED * P], U32, align_bytes=64)
        neg_scales = consts.tile([P, N_PAIRED * P], U8, align_bytes=64)

        sorted_of = {}
        grouped_of = {}
        codes_of = {}
        scales_of = {}
        excess_of = {}
        second_of = {}
        larger_of = {}
        plain_max = consts.tile([P, N_CHUNKS, N_PLAIN], F32)
        seq_max = consts.tile([P, BATCH, CHANNEL_TILES], F32)

        def sort_chunk(c):
            sorted_of[c] = {}
            for t in range(N_SORTED):
                sorted_of[c][t] = sort_pool.tile([P, 2, P], F32, name="sorted_words")
                nc.gpsimd.tensor_copy(
                    out=sorted_of[c][t][:],
                    in_=x_chunks[c][:, t, :].bitcast(F32).rearrange("p (m u) -> p u m", u=2),
                )

        def flip_chunk(c):
            grouped_of[c] = stage.tile([P, CHUNK, PACK], BF16, align_bytes=64, name="x_grouped")
            flip_rows(
                nc,
                psum,
                ident[:],
                x_chunks[c][:],
                grouped_of[c][:],
                CHUNK_ROW_TILES,
                sorted_of.get(c, {}),
            )

        def quantise_chunk(c):
            codes_of[c] = stage.tile([P, CHUNK], U32, align_bytes=64, name="x_codes")
            scales_of[c] = stage.tile([P, CHUNK], U8, align_bytes=64, name="x_scales")
            quantise(nc, grouped_of[c][:], codes_of[c][:], scales_of[c][:])

        def mx_pass(acc, weight_codes, weight_scales, c, start, stop):
            nc.tensor.matmul_mx(
                out=acc,
                lhsT=weight_codes.bitcast(FP8X4),
                lhsT_scale=weight_scales,
                rhs=codes_of[c][:].bitcast(FP8X4),
                rhs_scale=scales_of[c][:],
                start=start,
                stop=stop,
            )

        def multiply_plain(c):
            for t in range(N_PLAIN):
                channels = slice(t * P, (t + 1) * P)
                acc = psum.tile([P, CHUNK], F32, name="bank")
                mx_pass(acc[:], w_codes[:, channels], w_scales[:, channels], c, True, True)
                nc.vector.tensor_reduce(
                    out=plain_max[:, c, t : t + 1],
                    in_=acc[:],
                    axis=mybir.AxisListType.X,
                    op=ALU.max,
                )

        def multiply_paired(b, i):
            first, second = 2 * b, 2 * b + 1
            channels = slice((N_PLAIN + i) * P, (N_PLAIN + i + 1) * P)
            negated = slice(i * P, (i + 1) * P)
            difference = psum.tile([P, CHUNK], F32, name="bank")
            mx_pass(difference[:], w_codes[:, channels], w_scales[:, channels], first, True, False)
            mx_pass(difference[:], neg_codes[:, negated], neg_scales[:, negated], second, False, True)
            products = psum.tile([P, CHUNK], F32, name="bank")
            mx_pass(products[:], w_codes[:, channels], w_scales[:, channels], second, True, True)
            excess_of[b, i] = pair_in.tile([P, CHUNK], F32, name="excess")
            second_of[b, i] = pair_in.tile([P, CHUNK], F32, name="second_products")
            nc.scalar.activation(out=excess_of[b, i][:], in_=difference[:], func=FUNC.Relu)
            nc.scalar.copy(out=second_of[b, i][:], in_=products[:])

        def add_paired(b, i):
            larger_of[b, i] = pair_out.tile([P, CHUNK], F32, name="larger_%d" % i)
            nc.gpsimd.tensor_tensor(
                out=larger_of[b, i][:], in0=second_of[b, i][:], in1=excess_of[b, i][:], op=ALU.add
            )

        def reduce_paired(b, i):
            nc.vector.tensor_reduce(
                out=seq_max[:, b, N_PLAIN + i : N_PLAIN + i + 1],
                in_=larger_of[b, i][:],
                axis=mybir.AxisListType.X,
                op=ALU.max,
            )

        flip_chunk(0)
        flip_chunk(1)
        quantise_chunk(0)
        quantise_chunk(1)
        multiply_plain(0)
        nc.vector.tensor_scalar_mul(
            out=neg_grouped[:], in0=w_grouped[:, N_PLAIN * P :, :], scalar1=-1.0
        )
        quantise(nc, neg_grouped[:], neg_codes[:], neg_scales[:])
        flip_chunk(2)
        flip_chunk(3)
        bias_flipped = psum.tile([P, 2, PAIR], F32, name="bank")
        nc.tensor.transpose(bias_flipped[:, 0, 0:P], bias_rows_f32[:], ident[:])
        bias_col = consts.tile([P, CHANNEL_TILES], F32)
        nc.scalar.copy(out=bias_col[:], in_=bias_flipped[:, 0, 0:CHANNEL_TILES])
        for b in range(BATCH):
            if b + 2 < BATCH:
                sort_chunk(2 * b + 5)
            for i in range(N_PAIRED):
                multiply_paired(b, i)
            if b + 1 < BATCH:
                quantise_chunk(2 * b + 2)
                quantise_chunk(2 * b + 3)
            for i in range(N_PAIRED):
                if b >= 1:
                    reduce_paired(b - 1, i)
                add_paired(b, i)
            multiply_plain(2 * b + 1)
            if b + 1 < BATCH:
                multiply_plain(2 * b + 2)
            if b + 2 < BATCH:
                flip_chunk(2 * b + 4)
                flip_chunk(2 * b + 5)
        for i in range(N_PAIRED):
            reduce_paired(BATCH - 1, i)

        halves = plain_max[:].rearrange("p (b h) t -> p b h t", h=2)
        nc.vector.tensor_tensor(
            out=seq_max[:, :, 0:N_PLAIN], in0=halves[:, :, 0, :], in1=halves[:, :, 1, :], op=ALU.max
        )
        shape = [P, BATCH, CHANNEL_TILES]
        v = consts.tile(shape, F32)
        nc.vector.tensor_tensor(
            out=v[:], in0=seq_max[:], in1=bias_col[:].unsqueeze(1).to_broadcast(shape), op=ALU.add
        )
        negative = consts.tile(shape, F32)
        nc.vector.tensor_scalar_min(out=negative[:], in0=v[:], scalar1=0.0)
        nc.scalar.activation(out=negative[:], in_=negative[:], func=FUNC.Exp)
        positive = consts.tile(shape, F32)
        nc.vector.tensor_scalar_max(out=positive[:], in0=v[:], scalar1=0.0)
        nc.vector.scalar_tensor_tensor(
            out=result[:, 0 : BATCH * CHANNEL_TILES],
            in0=negative[:].rearrange("p b t -> p (b t)"),
            scalar=-1.0,
            in1=positive[:].rearrange("p b t -> p (b t)"),
            op0=ALU.add,
            op1=ALU.add,
        )

        result_flipped = psum.tile([P, 2, PAIR], F32, name="bank")
        nc.tensor.transpose(result_flipped[:, 0, 0:P], result[:], ident[:])
        out_rows = consts.tile([P, P], F32)
        nc.scalar.copy(out=out_rows[:], in_=result_flipped[:, 0, 0:P])
        nc.sync.dma_start(
            out=out.rearrange("b (t j) -> (b t) j", j=P),
            in_=out_rows[0 : BATCH * CHANNEL_TILES, :],
        )
